import numpy as np
import ml_dtypes


def mxq(x, axis, fmt="e4m3"):
    dtype, down = {"e4m3": (ml_dtypes.float8_e4m3fn, 7), "e5m2": (ml_dtypes.float8_e5m2, 14)}[fmt]
    v = np.moveaxis(np.asarray(x, np.float32).astype(ml_dtypes.bfloat16).astype(np.float64), axis, -1)
    blocks = v.reshape(v.shape[:-1] + (-1, 32))
    amax = np.abs(blocks).max(-1, keepdims=True)
    byte = np.maximum(np.where(amax > 0, np.frexp(amax)[1] - 1 + 127, 0) - down, 1)
    scale = np.exp2(byte - 127.0)
    codes = (blocks / scale).astype(np.float32).astype(dtype).astype(np.float64)
    return np.moveaxis((codes * scale).reshape(v.shape), -1, axis)


WIDE = False


def mx_kscale(k):
    if not WIDE:
        return np.ones(k)
    levels = np.array([10, -10, 5, -5, 0])
    a = np.random.permutation(np.resize(levels, k // 512 * 4)).reshape(k // 512, 4)
    idx = np.arange(k)
    return np.exp2(a[idx // 512, idx % 128 // 32])


BF16 = ml_dtypes.bfloat16


def bf(x):
    return np.asarray(x, np.float32).astype(BF16)


def f64(x):
    return np.asarray(x).astype(np.float64)


E2M1 = np.array([0.0, 0.5, 1.0, 1.5, 2.0, 3.0, 4.0, 6.0, -0.0, -0.5, -1.0, -1.5, -2.0, -3.0, -4.0, -6.0])


def pack_weight(w, fmt):
    k, n = w.shape
    w = f64(bf(w)).reshape(k // 32, 32, n)
    amax = np.abs(w).max(1)
    if fmt == "e4m3":
        byte = np.frexp(amax)[1] - 1 + 127 - 7
    else:
        mant, ex = np.frexp(amax / 6.0)
        byte = np.where(mant > 0.5, ex, ex - 1) + 127
    byte = np.clip(np.where(amax > 0, byte, 1), 1, 254)
    scaled = (w * np.exp2(127.0 - byte)[:, None, :]).reshape(k, n).astype(np.float32)
    by_word = np.ascontiguousarray(scaled.reshape(k // 512, 128, 4, n).transpose(0, 1, 3, 2))
    if fmt == "e4m3":
        words = by_word.astype(ml_dtypes.float8_e4m3fn).view(np.uint8)
    else:
        c = by_word.astype(ml_dtypes.float4_e2m1fn).view(np.uint8) & 0xF
        words = c[..., 0::2] | (c[..., 1::2] << 4)
    return np.ascontiguousarray(words), np.ascontiguousarray(byte.astype(np.uint8).reshape(k // 512, 16, n))


def unpack_weight(words, scales, fmt):
    g, p, n, _ = words.shape
    if fmt == "e4m3":
        vals = np.ascontiguousarray(words).view(ml_dtypes.float8_e4m3fn).astype(np.float64)
    else:
        nib = np.empty((g, p, n, 4), np.uint8)
        nib[..., 0::2] = words & 0xF
        nib[..., 1::2] = words >> 4
        vals = E2M1[nib]
    vals = vals * np.repeat(np.exp2(scales.astype(np.float64) - 127.0), 8, axis=1)[..., None]
    return vals.transpose(0, 1, 3, 2).reshape(g * 512, n)


B, F_IN, HID, E, G, H = 4096, 64, 1024, 32, 4, 8
BN_EPS = 1e-5
L1_EPS = 1e-6 ** 2
SELU_ALPHA = 1.6732632423543772
SELU_SCALE = 1.0507009873554805


def selu(v):
    return SELU_SCALE * np.where(v > 0.0, v, SELU_ALPHA * (np.exp(np.minimum(v, 0.0)) - 1.0))


def setup_inputs():
    s = mx_kscale(HID)
    t = s / s.min()
    col_std = 0.5 + np.random.random(HID)
    col_mean = 0.5 * np.random.standard_normal(HID)
    h2 = bf(np.random.standard_normal((B, HID)) * col_std + col_mean)
    gamma = bf((1.0 + 0.1 * np.random.standard_normal(HID)) * t)
    beta = bf(0.1 * np.random.standard_normal(HID) * t)
    stack = np.random.standard_normal((H, G, HID, E)) / np.sqrt(HID) / t[:, None]
    words, scales = pack_weight(stack.reshape(-1, E), "e4m3")
    bh = bf(0.3 * np.random.standard_normal((H, G, E)))
    return {"h2": h2,
            "gamma": gamma,
            "beta": beta,
            "Wh_words": words,
            "Wh_scales": scales,
            "bh": bh}


def reference(h2, gamma, beta, Wh_words, Wh_scales, bh):
    h2 = f64(h2)
    mu = h2.mean(axis=0)
    var = h2.var(axis=0)
    e = selu((h2 - mu) / np.sqrt(var + BN_EPS) * f64(gamma) + f64(beta))
    p = (mxq(e, 1, "e4m3") @ unpack_weight(Wh_words, Wh_scales, "e4m3").reshape(H, G, HID, E)).transpose(2, 0, 1, 3)
    d = selu(p + f64(bh))
    a = np.abs(d)
    l1 = np.maximum(a.sum(axis=-1, keepdims=True), L1_EPS)
    return np.sign(d) * (a / l1)

@@ -1,0 +1,281 @@
+import math
+from contextlib import ExitStack
+
+import concourse.mybir as mybir
+from concourse.masks import make_identity
+
+F32 = mybir.dt.float32
+BF16 = mybir.dt.bfloat16
+I32 = mybir.dt.int32
+U32 = mybir.dt.uint32
+U8 = mybir.dt.uint8
+FP8X4 = mybir.dt.float8_e4m3fn_x4
+ACT = mybir.ActivationFunctionType
+ALU = mybir.AluOpType
+AXIS = mybir.AxisListType
+
+P = 128
+ROWS = 4096
+FEATURES = 1024
+OUTPUTS = 1024
+HEAD = 32
+PACK = 4
+K_PASS = P * PACK
+PASSES = FEATURES // K_PASS
+BLOCK = 512
+SUBS = BLOCK // P
+N_BLOCKS = ROWS // BLOCK
+OUT_TILES = OUTPUTS // P
+HALF_TILES = OUT_TILES // 2
+STAT_CHUNK = 512
+
+BN_EPS = 1e-5
+L1_EPS = 1e-12
+SELU_ALPHA = 1.6732632423543772
+SELU_SCALE = 1.0507009873554805
+SCALE_ALPHA = SELU_SCALE * SELU_ALPHA
+
+FLOPS = 2 * ROWS * FEATURES * OUTPUTS
+
+
+def tile_basicemotionpredictions_pa_t_e_kernel(tc, h2, gamma, beta, Wh_words, Wh_scales, bh, out):
+    nc = tc.nc
+    out_rows = out.rearrange("b h g e -> b (h g e)")
+
+    with ExitStack() as ctx:
+        const = ctx.enter_context(tc.tile_pool(name="const", bufs=1))
+        xpool = ctx.enter_context(tc.tile_pool(name="x", bufs=1))
+        act1 = ctx.enter_context(tc.tile_pool(name="act1", bufs=2))
+        quant = ctx.enter_context(tc.tile_pool(name="quant", bufs=4))
+        act2 = ctx.enter_context(tc.tile_pool(name="act2", bufs=3))
+        dpool = ctx.enter_context(tc.tile_pool(name="d", bufs=OUT_TILES))
+        opool = ctx.enter_context(tc.tile_pool(name="o", bufs=4))
+        small = ctx.enter_context(tc.tile_pool(name="small", bufs=4))
+        xt_psum = ctx.enter_context(tc.psum_pool(name="xt_psum", bufs=2))
+        pm_psum = ctx.enter_context(tc.psum_pool(name="pm_psum", bufs=3))
+        tb_psum = ctx.enter_context(tc.psum_pool(name="tb_psum", bufs=3))
+
+        x_blocks = []
+        for blk in range(N_BLOCKS):
+            x_blk = xpool.tile([P, SUBS, FEATURES], BF16, name="x%d" % blk)
+            nc.sync.dma_start(
+                out=x_blk[:],
+                in_=h2[blk * BLOCK : (blk + 1) * BLOCK, :].rearrange("(p s) k -> p s k", s=SUBS),
+            )
+            x_blocks.append(x_blk)
+
+        gamma_bf = const.tile([P, PASSES, PACK], BF16)
+        beta_bf = const.tile([P, PASSES, PACK], BF16)
+        nc.scalar.dma_start(out=gamma_bf[:], in_=gamma.rearrange("(c p t) -> p c t", c=PASSES, t=PACK))
+        nc.scalar.dma_start(out=beta_bf[:], in_=beta.rearrange("(c p t) -> p c t", c=PASSES, t=PACK))
+        bh_bf = const.tile([P, OUT_TILES], BF16)
+        with nc.allow_non_contiguous_dma(reason="1,024 bias values, one to a partition and column"):
+            nc.scalar.dma_start(out=bh_bf[:], in_=bh.rearrange("h g e -> (h g e)").rearrange("(j p) -> p j", p=P))
+
+        ident = const.tile([P, P], F32)
+        make_identity(nc, ident[:])
+
+        w_words = const.tile([P, PASSES, OUTPUTS], U32, align_bytes=64)
+        w_planes = const.tile([P, PASSES, OUTPUTS], U8, align_bytes=64)
+        nc.vector.memset(w_planes[:].rearrange("p c n -> p (c n)").bitcast(I32), 0)
+        words_dram = Wh_words.rearrange("g p n t -> g p (n t)").bitcast(I32).rearrange("(m c) p n -> c p m n", c=PASSES)
+        scales_dram = Wh_scales.bitcast(I32).rearrange("(m c) q w -> c q m w", c=PASSES)
+        for c in range(PASSES):
+            nc.sync.dma_start(
+                out=w_words[:, c, :].bitcast(I32).rearrange("p (m n) -> p m n", n=HEAD),
+                in_=words_dram[c],
+            )
+        for c in range(PASSES):
+            for quad in range(4):
+                nc.sync.dma_start(
+                    out=w_planes[32 * quad : 32 * quad + 4, c, :].bitcast(I32).rearrange("r (m w) -> r m w", w=HEAD // 4),
+                    in_=scales_dram[c, 4 * quad : 4 * quad + 4],
+                )
+
+        warm_in = const.tile([P, 1], F32)
+        warm_sqrt = const.tile([P, 1], F32)
+        warm_exp = const.tile([P, 1], F32)
+        nc.vector.memset(warm_in[:], 1.0)
+        nc.scalar.activation(out=warm_sqrt[:], in_=warm_in[:], func=ACT.Sqrt)
+
+        def transpose_features(blk, c, u):
+            x_words = x_blocks[blk][:].bitcast(F32)
+            xt = xt_psum.tile([P, BLOCK], F32, name="xt")
+            for s in range(SUBS):
+                nc.tensor.transpose(
+                    out=xt[:, s * P : (s + 1) * P],
+                    in_=x_words[:, s, 256 * c + u : 256 * (c + 1) : 2],
+                    identity=ident[:],
+                )
+            return xt
+
+        chunks = N_BLOCKS * 2 * BLOCK // STAT_CHUNK
+        stats = const.tile([P, 2 * PASSES, chunks, 6], F32)
+        for blk in range(N_BLOCKS):
+            for c in range(PASSES):
+                for u in range(2):
+                    xt = transpose_features(blk, c, u)
+                    pairs = xt[:].bitcast(BF16)
+                    for h in range(2):
+                        nc.vector.bn_stats(
+                            out=stats[:, 2 * c + u, 2 * blk + h, :],
+                            in_=pairs[:, h * STAT_CHUNK : (h + 1) * STAT_CHUNK],
+                        )
+        n_feat = PASSES * PACK
+        mean_var = const.tile([P, n_feat, 2], F32)
+        for cu in range(2 * PASSES):
+            for e in range(2):
+                nc.vector.bn_aggr(out=mean_var[:, 2 * cu + e, :], in_=stats[:, cu, :, 3 * e : 3 * e + 3])
+
+        var_eps = const.tile([P, n_feat], F32)
+        std = const.tile([P, n_feat], F32)
+        rstd = const.tile([P, n_feat], F32)
+        gain = const.tile([P, n_feat], F32)
+        mean_gain = const.tile([P, n_feat], F32)
+        shift = const.tile([P, n_feat], F32)
+        lin_scale = const.tile([P, n_feat], F32)
+        lin_bias = const.tile([P, n_feat], F32)
+        zero = const.tile([P, 1], F32)
+        exp1_bias = const.tile([P, 1], F32)
+        nc.vector.tensor_scalar_add(out=var_eps[:], in0=mean_var[:, :, 1], scalar1=BN_EPS)
+        nc.scalar.activation(out=std[:], in_=var_eps[:], func=ACT.Sqrt)
+        nc.scalar.activation(out=warm_exp[:], in_=std[:, 0:1], func=ACT.Exp)
+        nc.vector.reciprocal(out=rstd[:], in_=std[:])
+        nc.vector.tensor_mul(out=gain[:], in0=rstd[:], in1=gamma_bf[:].rearrange("p c t -> p (c t)"))
+        nc.vector.tensor_mul(out=mean_gain[:], in0=mean_var[:, :, 0], in1=gain[:])
+        nc.vector.tensor_sub(out=shift[:], in0=beta_bf[:].rearrange("p c t -> p (c t)"), in1=mean_gain[:])
+        nc.vector.tensor_scalar_mul(out=lin_scale[:], in0=gain[:], scalar1=SELU_SCALE)
+        nc.vector.tensor_scalar(
+            out=lin_bias[:], in0=shift[:], scalar1=SELU_SCALE, scalar2=-SCALE_ALPHA, op0=ALU.mult, op1=ALU.add,
+        )
+        nc.vector.memset(zero[:], 0.0)
+        nc.vector.tensor_scalar_add(out=exp1_bias[:], in0=zero[:], scalar1=SELU_ALPHA + math.log(SCALE_ALPHA))
+
+        relu2_bias = const.tile([P, OUT_TILES], F32)
+        exp2_bias = const.tile([P, OUT_TILES], F32)
+        nc.vector.tensor_copy(out=relu2_bias[:], in_=bh_bf[:])
+        nc.vector.tensor_scalar_add(out=exp2_bias[:], in0=bh_bf[:], scalar1=math.log(SELU_ALPHA))
+
+        branches = {}
+        clamped = {}
+        exps = {}
+        e_mx = {}
+        d_tiles = {}
+
+        def linear_branch(blk, c, u):
+            if u == 0:
+                lin = act1.tile([P, PACK, BLOCK], F32, name="lin")
+                branches[(blk, c)] = lin
+            lin = branches[(blk, c)]
+            xt = transpose_features(blk, c, u)
+            pairs = xt[:].bitcast(BF16).rearrange("p (b e) -> p b e", e=2)
+            for e in range(2):
+                t = 2 * u + e
+                f = PACK * c + t
+                nc.scalar.activation(
+                    out=lin[:, t, :], in_=pairs[:, :, e], func=ACT.Identity,
+                    bias=lin_bias[:, f : f + 1], scale=lin_scale[:, f : f + 1],
+                )
+
+        def clamp(blk, c):
+            neg = act1.tile([P, BLOCK, PACK], F32, name="neg")
+            nc.vector.tensor_scalar_min(
+                out=neg[:], in0=branches[(blk, c)][:].rearrange("p t b -> p b t"), scalar1=-SCALE_ALPHA,
+            )
+            clamped[(blk, c)] = neg
+
+        def exp_branch(blk, c):
+            expo = act1.tile([P, BLOCK, PACK], F32, name="expo")
+            nc.scalar.activation(
+                out=expo[:], in_=clamped[(blk, c)][:], func=ACT.Exp, bias=exp1_bias[:, 0:1], scale=1.0 / SELU_SCALE,
+            )
+            exps[(blk, c)] = expo
+
+        def quantise_e(blk, c):
+            grouped = act1.tile([P, BLOCK, PACK], BF16, name="grouped", align_bytes=64)
+            nc.vector.scalar_tensor_tensor(
+                out=grouped[:],
+                in0=branches[(blk, c)][:].rearrange("p t b -> p b t"),
+                scalar=-SCALE_ALPHA,
+                in1=exps[(blk, c)][:],
+                op0=ALU.max,
+                op1=ALU.add,
+            )
+            e_words = quant.tile([P, BLOCK], U32, name="e_words", align_bytes=64)
+            e_plane = quant.tile([P, BLOCK], U8, name="e_plane", align_bytes=64)
+            nc.vector.quantize_mx(
+                out=e_words[:].bitcast(FP8X4),
+                scales=e_plane[:],
+                in_=grouped[:].rearrange("p b t -> p (b t)"),
+            )
+            e_mx[(blk, c)] = (e_words, e_plane)
+
+        def heads(blk, j):
+            cols = slice(j * P, (j + 1) * P)
+            pm = pm_psum.tile([P, BLOCK], F32, name="pm")
+            for c in range(PASSES):
+                e_words, e_plane = e_mx[(blk, c)]
+                nc.tensor.matmul_mx(
+                    out=pm[:],
+                    lhsT=w_words[:, c, cols].bitcast(FP8X4),
+                    lhsT_scale=w_planes[:, c, cols],
+                    rhs=e_words[:].bitcast(FP8X4),
+                    rhs_scale=e_plane[:],
+                    start=(c == 0),
+                    stop=(c == PASSES - 1),
+                )
+            exp2 = act2.tile([P, BLOCK], F32, name="exp2")
+            relu2 = act2.tile([P, BLOCK], F32, name="relu2")
+            nc.scalar.activation(out=exp2[:], in_=pm[:], func=ACT.Exp, bias=exp2_bias[:, j : j + 1], scale=1.0)
+            nc.scalar.activation(out=relu2[:], in_=pm[:], func=ACT.Relu, bias=relu2_bias[:, j : j + 1], scale=1.0)
+            d = dpool.tile([P, BLOCK], F32, name="d")
+            nc.vector.scalar_tensor_tensor(
+                out=d[:], in0=exp2[:], scalar=-SELU_ALPHA, in1=relu2[:], op0=ALU.add, op1=ALU.min,
+            )
+            d_tiles[(blk, j)] = d
+
+        def normalise_and_store(blk, half, s):
+            tb = tb_psum.tile([P, HALF_TILES * P], F32, name="tb")
+            for jj in range(HALF_TILES):
+                nc.tensor.transpose(
+                    out=tb[:, jj * P : (jj + 1) * P],
+                    in_=d_tiles[(blk, half * HALF_TILES + jj)][:, s * P : (s + 1) * P],
+                    identity=ident[:],
+                )
+            n_heads = HALF_TILES * P // HEAD
+            by_head = tb[:].rearrange("p (m e) -> p m e", e=HEAD)
+            l1 = small.tile([P, n_heads], F32, name="l1")
+            l1_floor = small.tile([P, n_heads], F32, name="l1_floor")
+            inv = small.tile([P, n_heads], F32, name="inv")
+            magnitudes = opool.tile([P, n_heads, HEAD], F32, name="magnitudes")
+            nc.scalar.activation(out=magnitudes[:], in_=by_head, func=ACT.Abs)
+            nc.vector.tensor_reduce(out=l1[:], in_=magnitudes[:], axis=AXIS.X, op=ALU.add)
+            nc.vector.tensor_scalar_max(out=l1_floor[:], in0=l1[:], scalar1=L1_EPS / SELU_SCALE)
+            nc.vector.reciprocal(out=inv[:], in_=l1_floor[:])
+            o = opool.tile([P, n_heads, HEAD], F32, name="o")
+            nc.vector.tensor_tensor(
+                out=o[:], in0=by_head, in1=inv[:].unsqueeze(2).to_broadcast([P, n_heads, HEAD]), op=ALU.mult,
+            )
+            rows = out_rows[blk * BLOCK : (blk + 1) * BLOCK, :].rearrange("(p s) n -> p s n", s=SUBS)
+            nc.sync.dma_start(
+                out=rows[:, s, half * HALF_TILES * P : (half + 1) * HALF_TILES * P],
+                in_=o[:].rearrange("p m e -> p (m e)"),
+            )
+
+        for blk in range(-1, N_BLOCKS + 1):
+            nxt = blk + 1
+            for j in range(OUT_TILES):
+                if j % 4 < 2 and nxt < N_BLOCKS:
+                    linear_branch(nxt, j // 4, j % 4)
+                if j % 4 == 1 and nxt < N_BLOCKS:
+                    clamp(nxt, j // 4)
+                if j % 4 == 2 and nxt < N_BLOCKS:
+                    exp_branch(nxt, j // 4)
+                if 0 <= blk < N_BLOCKS:
+                    heads(blk, j)
+                if j % 4 == 3 and nxt < N_BLOCKS:
+                    quantise_e(nxt, j // 4)
+                if j >= HALF_TILES and 0 <= blk < N_BLOCKS:
+                    normalise_and_store(blk, 0, j - HALF_TILES)
+                if j < HALF_TILES and 0 <= blk - 1:
+                    normalise_and_store(blk - 1, 1, j)

@@ -51,9 +51,10 @@ def tile_basicemotionpredictions_pa_t_e_kernel(tc, h2, gamma, beta, Wh_words, Wh
         dpool = ctx.enter_context(tc.tile_pool(name="d", bufs=OUT_TILES))
         opool = ctx.enter_context(tc.tile_pool(name="o", bufs=4))
         small = ctx.enter_context(tc.tile_pool(name="small", bufs=4))
+        scrap = ctx.enter_context(tc.tile_pool(name="scrap", bufs=4))
         xt_psum = ctx.enter_context(tc.psum_pool(name="xt_psum", bufs=2))
-        pm_psum = ctx.enter_context(tc.psum_pool(name="pm_psum", bufs=3))
-        tb_psum = ctx.enter_context(tc.psum_pool(name="tb_psum", bufs=3))
+        pm_psum = ctx.enter_context(tc.psum_pool(name="pm_psum", bufs=2))
+        tb_psum = ctx.enter_context(tc.psum_pool(name="tb_psum", bufs=4))
 
         x_blocks = []
         for blk in range(N_BLOCKS):
@@ -98,9 +99,9 @@ def tile_basicemotionpredictions_pa_t_e_kernel(tc, h2, gamma, beta, Wh_words, Wh
         nc.vector.memset(warm_in[:], 1.0)
         nc.scalar.activation(out=warm_sqrt[:], in_=warm_in[:], func=ACT.Sqrt)
 
-        def transpose_features(blk, c, u):
+        def transpose_features(blk, c, u, pool, tag):
             x_words = x_blocks[blk][:].bitcast(F32)
-            xt = xt_psum.tile([P, BLOCK], F32, name="xt")
+            xt = pool.tile([P, BLOCK], F32, name="xt", tag=tag)
             for s in range(SUBS):
                 nc.tensor.transpose(
                     out=xt[:, s * P : (s + 1) * P],
@@ -110,22 +111,51 @@ def tile_basicemotionpredictions_pa_t_e_kernel(tc, h2, gamma, beta, Wh_words, Wh
             return xt
 
         chunks = N_BLOCKS * 2 * BLOCK // STAT_CHUNK
-        stats = const.tile([P, 2 * PASSES, chunks, 6], F32)
+        vector_banks = 2 * PASSES - 1
+        n_feat = PASSES * PACK
+        stats = const.tile([P, vector_banks, chunks, 6], F32)
+        neg_pivot = const.tile([P, 2], F32)
+        sums = const.tile([P, 2, 2, N_BLOCKS], F32)
         for blk in range(N_BLOCKS):
             for c in range(PASSES):
                 for u in range(2):
-                    xt = transpose_features(blk, c, u)
+                    if 2 * c + u < vector_banks:
+                        xt = transpose_features(blk, c, u, xt_psum, "xt")
+                    else:
+                        xt = transpose_features(blk, c, u, tb_psum, "tb")
                     pairs = xt[:].bitcast(BF16)
-                    for h in range(2):
-                        nc.vector.bn_stats(
-                            out=stats[:, 2 * c + u, 2 * blk + h, :],
-                            in_=pairs[:, h * STAT_CHUNK : (h + 1) * STAT_CHUNK],
-                        )
-        n_feat = PASSES * PACK
+                    if 2 * c + u < vector_banks:
+                        for h in range(2):
+                            nc.vector.bn_stats(
+                                out=stats[:, 2 * c + u, 2 * blk + h, :],
+                                in_=pairs[:, h * STAT_CHUNK : (h + 1) * STAT_CHUNK],
+                            )
+                    else:
+                        if blk == 0:
+                            nc.vector.tensor_scalar_mul(out=neg_pivot[:], in0=pairs[:, 0:2], scalar1=-1.0)
+                        by_feature = pairs.rearrange("p (b e) -> p b e", e=2)
+                        for e in range(2):
+                            centred = scrap.tile([P, BLOCK], BF16, name="centred")
+                            squared = scrap.tile([P, BLOCK], BF16, name="squared")
+                            nc.scalar.activation(
+                                out=centred[:], in_=by_feature[:, :, e], func=ACT.Identity,
+                                bias=neg_pivot[:, e : e + 1], scale=1.0, accum_out=sums[:, e, 0, blk : blk + 1],
+                            )
+                            nc.scalar.activation(
+                                out=squared[:], in_=by_feature[:, :, e], func=ACT.Square,
+                                bias=neg_pivot[:, e : e + 1], scale=1.0, accum_out=sums[:, e, 1, blk : blk + 1],
+                            )
         mean_var = const.tile([P, n_feat, 2], F32)
-        for cu in range(2 * PASSES):
+        for cu in range(vector_banks):
             for e in range(2):
                 nc.vector.bn_aggr(out=mean_var[:, 2 * cu + e, :], in_=stats[:, cu, :, 3 * e : 3 * e + 3])
+        moments = const.tile([P, 2, 2], F32)
+        m1_squared = const.tile([P, 2], F32)
+        nc.vector.tensor_reduce(out=moments[:], in_=sums[:], axis=AXIS.X, op=ALU.add)
+        nc.vector.tensor_scalar_mul(out=moments[:], in0=moments[:], scalar1=1.0 / ROWS)
+        nc.vector.tensor_sub(out=mean_var[:, 2 * vector_banks :, 0], in0=moments[:, :, 0], in1=neg_pivot[:])
+        nc.vector.tensor_mul(out=m1_squared[:], in0=moments[:, :, 0], in1=moments[:, :, 0])
+        nc.vector.tensor_sub(out=mean_var[:, 2 * vector_banks :, 1], in0=moments[:, :, 1], in1=m1_squared[:])
 
         var_eps = const.tile([P, n_feat], F32)
         std = const.tile([P, n_feat], F32)
@@ -167,7 +197,7 @@ def tile_basicemotionpredictions_pa_t_e_kernel(tc, h2, gamma, beta, Wh_words, Wh
                 lin = act1.tile([P, PACK, BLOCK], F32, name="lin")
                 branches[(blk, c)] = lin
             lin = branches[(blk, c)]
-            xt = transpose_features(blk, c, u)
+            xt = transpose_features(blk, c, u, xt_psum, "xt")
             pairs = xt[:].bitcast(BF16).rearrange("p (b e) -> p b e", e=2)
             for e in range(2):
                 t = 2 * u + e
@@ -234,33 +264,37 @@ def tile_basicemotionpredictions_pa_t_e_kernel(tc, h2, gamma, beta, Wh_words, Wh
             )
             d_tiles[(blk, j)] = d
 
-        def normalise_and_store(blk, half, s):
-            tb = tb_psum.tile([P, HALF_TILES * P], F32, name="tb")
-            for jj in range(HALF_TILES):
-                nc.tensor.transpose(
-                    out=tb[:, jj * P : (jj + 1) * P],
-                    in_=d_tiles[(blk, half * HALF_TILES + jj)][:, s * P : (s + 1) * P],
-                    identity=ident[:],
-                )
+        def normalise_and_store(blk, half, pair):
             n_heads = HALF_TILES * P // HEAD
-            by_head = tb[:].rearrange("p (m e) -> p m e", e=HEAD)
-            l1 = small.tile([P, n_heads], F32, name="l1")
-            l1_floor = small.tile([P, n_heads], F32, name="l1_floor")
-            inv = small.tile([P, n_heads], F32, name="inv")
-            magnitudes = opool.tile([P, n_heads, HEAD], F32, name="magnitudes")
-            nc.scalar.activation(out=magnitudes[:], in_=by_head, func=ACT.Abs)
+            rows = out_rows[blk * BLOCK : (blk + 1) * BLOCK, :].rearrange("(p s) n -> p s n", s=SUBS)
+            magnitudes = opool.tile([P, 2, n_heads, HEAD], F32, name="magnitudes")
+            banks = []
+            for i in range(2):
+                s = 2 * pair + i
+                tb = tb_psum.tile([P, n_heads, HEAD], F32, name="tb", tag="tb")
+                for jj in range(HALF_TILES):
+                    nc.tensor.transpose(
+                        out=tb[:].rearrange("p m e -> p (m e)")[:, jj * P : (jj + 1) * P],
+                        in_=d_tiles[(blk, half * HALF_TILES + jj)][:, s * P : (s + 1) * P],
+                        identity=ident[:],
+                    )
+                nc.scalar.activation(out=magnitudes[:, i], in_=tb[:], func=ACT.Abs)
+                banks.append(tb)
+            l1 = small.tile([P, 2, n_heads], F32, name="l1")
+            l1_floor = small.tile([P, 2, n_heads], F32, name="l1_floor")
+            inv = small.tile([P, 2, n_heads], F32, name="inv")
             nc.vector.tensor_reduce(out=l1[:], in_=magnitudes[:], axis=AXIS.X, op=ALU.add)
             nc.vector.tensor_scalar_max(out=l1_floor[:], in0=l1[:], scalar1=L1_EPS / SELU_SCALE)
             nc.vector.reciprocal(out=inv[:], in_=l1_floor[:])
-            o = opool.tile([P, n_heads, HEAD], F32, name="o")
-            nc.vector.tensor_tensor(
-                out=o[:], in0=by_head, in1=inv[:].unsqueeze(2).to_broadcast([P, n_heads, HEAD]), op=ALU.mult,
-            )
-            rows = out_rows[blk * BLOCK : (blk + 1) * BLOCK, :].rearrange("(p s) n -> p s n", s=SUBS)
-            nc.sync.dma_start(
-                out=rows[:, s, half * HALF_TILES * P : (half + 1) * HALF_TILES * P],
-                in_=o[:].rearrange("p m e -> p (m e)"),
-            )
+            for i in range(2):
+                o = opool.tile([P, n_heads, HEAD], F32, name="o")
+                nc.vector.tensor_tensor(
+                    out=o[:], in0=banks[i][:], in1=inv[:, i].unsqueeze(2).to_broadcast([P, n_heads, HEAD]), op=ALU.mult,
+                )
+                nc.sync.dma_start(
+                    out=rows[:, 2 * pair + i, half * HALF_TILES * P : (half + 1) * HALF_TILES * P],
+                    in_=o[:].rearrange("p m e -> p (m e)"),
+                )
 
         for blk in range(-1, N_BLOCKS + 1):
             nxt = blk + 1
@@ -275,7 +309,7 @@ def tile_basicemotionpredictions_pa_t_e_kernel(tc, h2, gamma, beta, Wh_words, Wh
                     heads(blk, j)
                 if j % 4 == 3 and nxt < N_BLOCKS:
                     quantise_e(nxt, j // 4)
-                if j >= HALF_TILES and 0 <= blk < N_BLOCKS:
-                    normalise_and_store(blk, 0, j - HALF_TILES)
-                if j < HALF_TILES and 0 <= blk - 1:
-                    normalise_and_store(blk - 1, 1, j)
+                if j % 2 == 1 and j >= HALF_TILES and 0 <= blk < N_BLOCKS:
+                    normalise_and_store(blk, 0, (j - HALF_TILES) // 2)
+                if j % 2 == 1 and j < HALF_TILES and 0 <= blk - 1:
+                    normalise_and_store(blk - 1, 1, j // 2)

@@ -208,14 +208,12 @@ def tile_basicemotionpredictions_pa_t_e_kernel(tc, h2, gamma, beta, Wh_words, Wh
                 )
 
         def clamp(blk, c):
-            neg = act1.tile([P, BLOCK, PACK], F32, name="neg")
-            nc.vector.tensor_scalar_min(
-                out=neg[:], in0=branches[(blk, c)][:].rearrange("p t b -> p b t"), scalar1=-SCALE_ALPHA,
-            )
+            neg = act1.tile([P, PACK, BLOCK], F32, name="neg")
+            nc.vector.tensor_scalar_min(out=neg[:], in0=branches[(blk, c)][:], scalar1=-SCALE_ALPHA)
             clamped[(blk, c)] = neg
 
         def exp_branch(blk, c):
-            expo = act1.tile([P, BLOCK, PACK], F32, name="expo")
+            expo = act1.tile([P, PACK, BLOCK], F32, name="expo")
             nc.scalar.activation(
                 out=expo[:], in_=clamped[(blk, c)][:], func=ACT.Exp, bias=exp1_bias[:, 0:1], scale=1.0 / SELU_SCALE,
             )
@@ -227,7 +225,7 @@ def tile_basicemotionpredictions_pa_t_e_kernel(tc, h2, gamma, beta, Wh_words, Wh
                 out=grouped[:],
                 in0=branches[(blk, c)][:].rearrange("p t b -> p b t"),
                 scalar=-SCALE_ALPHA,
-                in1=exps[(blk, c)][:],
+                in1=exps[(blk, c)][:].rearrange("p t b -> p b t"),
                 op0=ALU.max,
                 op1=ALU.add,
             )

@@ -27,6 +27,8 @@ SUBS = BLOCK // P
 N_BLOCKS = ROWS // BLOCK
 OUT_TILES = OUTPUTS // P
 HALF_TILES = OUT_TILES // 2
+HEADS = OUTPUTS // HEAD
+E_LOW = HEAD // OUT_TILES
 STAT_CHUNK = 512
 
 BN_EPS = 1e-5
@@ -47,17 +49,19 @@ def tile_basicemotionpredictions_pa_t_e_kernel(tc, h2, gamma, beta, Wh_words, Wh
         xpool = ctx.enter_context(tc.tile_pool(name="x", bufs=1))
         act1 = ctx.enter_context(tc.tile_pool(name="act1", bufs=2))
         quant = ctx.enter_context(tc.tile_pool(name="quant", bufs=4))
-        act2 = ctx.enter_context(tc.tile_pool(name="act2", bufs=3))
+        act2 = ctx.enter_context(tc.tile_pool(name="act2", bufs=2))
         dpool = ctx.enter_context(tc.tile_pool(name="d", bufs=OUT_TILES))
-        opool = ctx.enter_context(tc.tile_pool(name="o", bufs=4))
-        small = ctx.enter_context(tc.tile_pool(name="small", bufs=4))
+        opool = ctx.enter_context(tc.tile_pool(name="o", bufs=3))
+        small = ctx.enter_context(tc.tile_pool(name="small", bufs=2))
         scrap = ctx.enter_context(tc.tile_pool(name="scrap", bufs=4))
         xt_psum = ctx.enter_context(tc.psum_pool(name="xt_psum", bufs=2))
         pm_psum = ctx.enter_context(tc.psum_pool(name="pm_psum", bufs=2))
-        tb_psum = ctx.enter_context(tc.psum_pool(name="tb_psum", bufs=4))
+        sum_psum = ctx.enter_context(tc.psum_pool(name="sum_psum", bufs=1))
+        tv_psum = ctx.enter_context(tc.psum_pool(name="tv_psum", bufs=2))
 
         x_blocks = []
-        for blk in range(N_BLOCKS):
+
+        def load_x(blk):
             x_blk = xpool.tile([P, SUBS, FEATURES], BF16, name="x%d" % blk)
             nc.sync.dma_start(
                 out=x_blk[:],
@@ -65,33 +69,48 @@ def tile_basicemotionpredictions_pa_t_e_kernel(tc, h2, gamma, beta, Wh_words, Wh
             )
             x_blocks.append(x_blk)
 
+        for blk in range(4):
+            load_x(blk)
+
         gamma_bf = const.tile([P, PASSES, PACK], BF16)
         beta_bf = const.tile([P, PASSES, PACK], BF16)
         nc.scalar.dma_start(out=gamma_bf[:], in_=gamma.rearrange("(c p t) -> p c t", c=PASSES, t=PACK))
         nc.scalar.dma_start(out=beta_bf[:], in_=beta.rearrange("(c p t) -> p c t", c=PASSES, t=PACK))
         bh_bf = const.tile([P, OUT_TILES], BF16)
+        bh_heads = bh.rearrange("h g e -> (h g) e")
         with nc.allow_non_contiguous_dma(reason="1,024 bias values, one to a partition and column"):
-            nc.scalar.dma_start(out=bh_bf[:], in_=bh.rearrange("h g e -> (h g e)").rearrange("(j p) -> p j", p=P))
+            for e in range(E_LOW):
+                nc.scalar.dma_start(out=bh_bf[e:P:E_LOW, :], in_=bh_heads[:, e:HEAD:E_LOW])
 
         ident = const.tile([P, P], F32)
         make_identity(nc, ident[:])
 
+        w_raw = act1.tile([P, PASSES, OUTPUTS], I32, name="w_raw", tag="lin")
+        planes_raw = act1.tile([P, PASSES, OUTPUTS // 4], I32, name="planes_raw", tag="neg")
         w_words = const.tile([P, PASSES, OUTPUTS], U32, align_bytes=64)
         w_planes = const.tile([P, PASSES, OUTPUTS], U8, align_bytes=64)
-        nc.vector.memset(w_planes[:].rearrange("p c n -> p (c n)").bitcast(I32), 0)
+        nc.vector.memset(planes_raw[:].rearrange("p c n -> p (c n)"), 0)
         words_dram = Wh_words.rearrange("g p n t -> g p (n t)").bitcast(I32).rearrange("(m c) p n -> c p m n", c=PASSES)
         scales_dram = Wh_scales.bitcast(I32).rearrange("(m c) q w -> c q m w", c=PASSES)
         for c in range(PASSES):
-            nc.sync.dma_start(
-                out=w_words[:, c, :].bitcast(I32).rearrange("p (m n) -> p m n", n=HEAD),
-                in_=words_dram[c],
-            )
+            nc.sync.dma_start(out=w_raw[:, c, :].rearrange("p (m n) -> p m n", n=HEAD), in_=words_dram[c])
         for c in range(PASSES):
             for quad in range(4):
                 nc.sync.dma_start(
-                    out=w_planes[32 * quad : 32 * quad + 4, c, :].bitcast(I32).rearrange("r (m w) -> r m w", w=HEAD // 4),
+                    out=planes_raw[32 * quad : 32 * quad + 4, c, :].rearrange("r (m w) -> r m w", w=HEAD // 4),
                     in_=scales_dram[c, 4 * quad : 4 * quad + 4],
                 )
+        for blk in range(4, N_BLOCKS):
+            load_x(blk)
+        for c in range(PASSES):
+            nc.gpsimd.tensor_copy(
+                out=w_words[:, c, :].bitcast(I32).rearrange("p (j m e) -> p j m e", j=OUT_TILES, e=E_LOW),
+                in_=w_raw[:, c, :].rearrange("p (m j e) -> p j m e", j=OUT_TILES, e=E_LOW),
+            )
+            nc.gpsimd.tensor_copy(
+                out=w_planes[:, c, :].bitcast(I32).rearrange("p (j m) -> p j m", j=OUT_TILES),
+                in_=planes_raw[:, c, :].rearrange("p (m j) -> p j m", j=OUT_TILES),
+            )
 
         warm_in = const.tile([P, 1], F32)
         warm_sqrt = const.tile([P, 1], F32)
@@ -122,7 +141,7 @@ def tile_basicemotionpredictions_pa_t_e_kernel(tc, h2, gamma, beta, Wh_words, Wh
                     if 2 * c + u < vector_banks:
                         xt = transpose_features(blk, c, u, xt_psum, "xt")
                     else:
-                        xt = transpose_features(blk, c, u, tb_psum, "tb")
+                        xt = transpose_features(blk, c, u, tv_psum, "values")
                     pairs = xt[:].bitcast(BF16)
                     if 2 * c + u < vector_banks:
                         for h in range(2):
@@ -190,7 +209,10 @@ def tile_basicemotionpredictions_pa_t_e_kernel(tc, h2, gamma, beta, Wh_words, Wh
         clamped = {}
         exps = {}
         e_mx = {}
-        d_tiles = {}
+        pairs = {}
+        sums2 = {}
+        invs = {}
+        outs = {}
 
         def linear_branch(blk, c, u):
             if u == 0:
@@ -213,9 +235,9 @@ def tile_basicemotionpredictions_pa_t_e_kernel(tc, h2, gamma, beta, Wh_words, Wh
             clamped[(blk, c)] = neg
 
         def exp_branch(blk, c):
-            expo = act1.tile([P, PACK, BLOCK], F32, name="expo")
+            expo = clamped[(blk, c)]
             nc.scalar.activation(
-                out=expo[:], in_=clamped[(blk, c)][:], func=ACT.Exp, bias=exp1_bias[:, 0:1], scale=1.0 / SELU_SCALE,
+                out=expo[:], in_=expo[:], func=ACT.Exp, bias=exp1_bias[:, 0:1], scale=1.0 / SELU_SCALE,
             )
             exps[(blk, c)] = expo
 
@@ -252,50 +274,85 @@ def tile_basicemotionpredictions_pa_t_e_kernel(tc, h2, gamma, beta, Wh_words, Wh
                     start=(c == 0),
                     stop=(c == PASSES - 1),
                 )
-            exp2 = act2.tile([P, BLOCK], F32, name="exp2")
-            relu2 = act2.tile([P, BLOCK], F32, name="relu2")
-            nc.scalar.activation(out=exp2[:], in_=pm[:], func=ACT.Exp, bias=exp2_bias[:, j : j + 1], scale=1.0)
-            nc.scalar.activation(out=relu2[:], in_=pm[:], func=ACT.Relu, bias=relu2_bias[:, j : j + 1], scale=1.0)
-            d = dpool.tile([P, BLOCK], F32, name="d")
-            nc.vector.scalar_tensor_tensor(
-                out=d[:], in0=exp2[:], scalar=-SELU_ALPHA, in1=relu2[:], op0=ALU.add, op1=ALU.min,
+            if j % 2 == 0:
+                exp_pair = act2.tile([P, 2, BLOCK], F32, name="exp_pair")
+                pos_pair = dpool.tile([P, 2, BLOCK], F32, name="pos_pair")
+                cap_pair = dpool.tile([P, 2, BLOCK], F32, name="cap_pair")
+                pairs[(blk, j // 2)] = (pos_pair, cap_pair, exp_pair)
+            pos_pair, cap_pair, exp_pair = pairs[(blk, j // 2)]
+            nc.scalar.activation(
+                out=exp_pair[:, j % 2, :], in_=pm[:], func=ACT.Exp, bias=exp2_bias[:, j : j + 1], scale=1.0,
             )
-            d_tiles[(blk, j)] = d
+            nc.scalar.activation(
+                out=pos_pair[:, j % 2, :], in_=pm[:], func=ACT.Relu, bias=relu2_bias[:, j : j + 1], scale=1.0,
+            )
+            if j % 2 == 1:
+                nc.vector.tensor_scalar(
+                    out=cap_pair[:], in0=exp_pair[:], scalar1=SELU_ALPHA, scalar2=-SELU_ALPHA, op0=ALU.min, op1=ALU.add,
+                )
 
-        def normalise_and_store(blk, half, pair):
-            n_heads = HALF_TILES * P // HEAD
-            rows = out_rows[blk * BLOCK : (blk + 1) * BLOCK, :].rearrange("(p s) n -> p s n", s=SUBS)
-            magnitudes = opool.tile([P, 2, n_heads, HEAD], F32, name="magnitudes")
-            banks = []
-            for i in range(2):
-                s = 2 * pair + i
-                tb = tb_psum.tile([P, n_heads, HEAD], F32, name="tb", tag="tb")
-                for jj in range(HALF_TILES):
-                    nc.tensor.transpose(
-                        out=tb[:].rearrange("p m e -> p (m e)")[:, jj * P : (jj + 1) * P],
-                        in_=d_tiles[(blk, half * HALF_TILES + jj)][:, s * P : (s + 1) * P],
-                        identity=ident[:],
-                    )
-                nc.scalar.activation(out=magnitudes[:, i], in_=tb[:], func=ACT.Abs)
-                banks.append(tb)
-            l1 = small.tile([P, 2, n_heads], F32, name="l1")
-            l1_floor = small.tile([P, 2, n_heads], F32, name="l1_floor")
-            inv = small.tile([P, 2, n_heads], F32, name="inv")
-            nc.vector.tensor_reduce(out=l1[:], in_=magnitudes[:], axis=AXIS.X, op=ALU.add)
+        def turned(dest, blk, j, which, s, start, stop):
+            nc.tensor.matmul(
+                out=dest,
+                lhsT=pairs[(blk, j // 2)][which][:, j % 2, s * P : (s + 1) * P],
+                rhs=ident[:],
+                is_transpose=True,
+                start=start,
+                stop=stop,
+            )
+
+        def norm_sums(blk, s):
+            if s == 0:
+                sum_pos = sum_psum.tile([P, SUBS, P], F32, name="sum_pos")
+                sum_cap = sum_psum.tile([P, SUBS, P], F32, name="sum_cap")
+                sums2[blk] = (sum_pos, sum_cap)
+            for which in range(2):
+                for j in range(OUT_TILES):
+                    turned(sums2[blk][which][:, s, :], blk, j, which, s, j == 0, j == OUT_TILES - 1)
+
+        def norm_finish(blk):
+            sum_pos, sum_cap = sums2[blk]
+            l1_pos = small.tile([P, SUBS * HEADS], F32, name="l1_pos")
+            l1_cap = small.tile([P, SUBS * HEADS], F32, name="l1_cap")
+            l1 = small.tile([P, SUBS * HEADS], F32, name="l1")
+            l1_floor = small.tile([P, SUBS * HEADS], F32, name="l1_floor")
+            inv = small.tile([P, SUBS, HEADS], F32, name="inv")
+            nc.vector.tensor_reduce(
+                out=l1_pos[:], in_=sum_pos[:].rearrange("p s (m e) -> p (s m) e", e=E_LOW), axis=AXIS.X, op=ALU.add,
+            )
+            nc.vector.tensor_reduce(
+                out=l1_cap[:], in_=sum_cap[:].rearrange("p s (m e) -> p (s m) e", e=E_LOW), axis=AXIS.X, op=ALU.add,
+            )
+            nc.vector.tensor_sub(out=l1[:], in0=l1_pos[:], in1=l1_cap[:])
             nc.vector.tensor_scalar_max(out=l1_floor[:], in0=l1[:], scalar1=L1_EPS / SELU_SCALE)
-            nc.vector.reciprocal(out=inv[:], in_=l1_floor[:])
-            for i in range(2):
-                o = opool.tile([P, n_heads, HEAD], F32, name="o")
-                nc.vector.tensor_tensor(
-                    out=o[:], in0=banks[i][:], in1=inv[:, i].unsqueeze(2).to_broadcast([P, n_heads, HEAD]), op=ALU.mult,
-                )
-                nc.sync.dma_start(
-                    out=rows[:, 2 * pair + i, half * HALF_TILES * P : (half + 1) * HALF_TILES * P],
-                    in_=o[:].rearrange("p m e -> p (m e)"),
-                )
+            nc.vector.reciprocal(out=inv[:].rearrange("p s m -> p (s m)"), in_=l1_floor[:])
+            invs[blk] = inv
+
+        def normalise_and_store(blk, s, half):
+            rows = out_rows[blk * BLOCK : (blk + 1) * BLOCK, :].rearrange("(p s) n -> p s n", s=SUBS)
+            values = tv_psum.tile([P, HALF_TILES, HEADS, E_LOW], F32, name="values")
+            for jj in range(HALF_TILES):
+                for which in range(2):
+                    turned(
+                        values[:, jj].rearrange("p m e -> p (m e)"), blk, half * HALF_TILES + jj, which, s, which == 0, which == 1,
+                    )
+            if half == 0:
+                o = opool.tile([P, HEADS, HEAD], F32, name="o")
+                outs[(blk, s)] = o
+            o = outs[(blk, s)]
+            span = HALF_TILES * E_LOW
+            nc.vector.tensor_tensor(
+                out=o[:, :, half * span : (half + 1) * span].rearrange("p m (j e) -> p m j e", e=E_LOW),
+                in0=values[:].rearrange("p j m e -> p m j e"),
+                in1=invs[blk][:, s, :].unsqueeze(2).unsqueeze(3).to_broadcast([P, HEADS, HALF_TILES, E_LOW]),
+                op=ALU.mult,
+            )
+            if half == 1:
+                nc.sync.dma_start(out=rows[:, s, :], in_=o[:].rearrange("p m e -> p (m e)"))
 
         for blk in range(-1, N_BLOCKS + 1):
             nxt = blk + 1
+            prev = blk - 1
             for j in range(OUT_TILES):
                 if j % 4 < 2 and nxt < N_BLOCKS:
                     linear_branch(nxt, j // 4, j % 4)
@@ -307,7 +364,10 @@ def tile_basicemotionpredictions_pa_t_e_kernel(tc, h2, gamma, beta, Wh_words, Wh
                     heads(blk, j)
                 if j % 4 == 3 and nxt < N_BLOCKS:
                     quantise_e(nxt, j // 4)
-                if j % 2 == 1 and j >= HALF_TILES and 0 <= blk < N_BLOCKS:
-                    normalise_and_store(blk, 0, (j - HALF_TILES) // 2)
-                if j % 2 == 1 and j < HALF_TILES and 0 <= blk - 1:
-                    normalise_and_store(blk - 1, 1, j // 2)
+                if prev >= 0 and j < SUBS:
+                    norm_sums(prev, j)
+                if prev >= 0 and j == SUBS - 1:
+                    norm_finish(prev)
+                if prev >= 0 and j >= SUBS:
+                    normalise_and_store(prev, j - SUBS, 0)
+                    normalise_and_store(prev, j - SUBS, 1)

@@ -29,6 +29,7 @@ OUT_TILES = OUTPUTS // P
 HALF_TILES = OUT_TILES // 2
 HEADS = OUTPUTS // HEAD
 E_LOW = HEAD // OUT_TILES
+VECTOR_RELU_TILES = (0, 1, 2)
 STAT_CHUNK = 512
 
 BN_EPS = 1e-5
@@ -49,15 +50,15 @@ def tile_basicemotionpredictions_pa_t_e_kernel(tc, h2, gamma, beta, Wh_words, Wh
         xpool = ctx.enter_context(tc.tile_pool(name="x", bufs=1))
         act1 = ctx.enter_context(tc.tile_pool(name="act1", bufs=2))
         quant = ctx.enter_context(tc.tile_pool(name="quant", bufs=4))
-        act2 = ctx.enter_context(tc.tile_pool(name="act2", bufs=2))
+        act2 = ctx.enter_context(tc.tile_pool(name="act2", bufs=3))
         dpool = ctx.enter_context(tc.tile_pool(name="d", bufs=OUT_TILES))
+        wpool = ctx.enter_context(tc.tile_pool(name="w", bufs=6))
         opool = ctx.enter_context(tc.tile_pool(name="o", bufs=3))
         small = ctx.enter_context(tc.tile_pool(name="small", bufs=2))
         scrap = ctx.enter_context(tc.tile_pool(name="scrap", bufs=4))
         xt_psum = ctx.enter_context(tc.psum_pool(name="xt_psum", bufs=2))
         pm_psum = ctx.enter_context(tc.psum_pool(name="pm_psum", bufs=2))
-        sum_psum = ctx.enter_context(tc.psum_pool(name="sum_psum", bufs=1))
-        tv_psum = ctx.enter_context(tc.psum_pool(name="tv_psum", bufs=2))
+        tv_psum = ctx.enter_context(tc.psum_pool(name="tv_psum", bufs=4))
 
         x_blocks = []
 
@@ -275,21 +276,24 @@ def tile_basicemotionpredictions_pa_t_e_kernel(tc, h2, gamma, beta, Wh_words, Wh
                     stop=(c == PASSES - 1),
                 )
             if j % 2 == 0:
-                exp_pair = act2.tile([P, 2, BLOCK], F32, name="exp_pair")
-                pos_pair = dpool.tile([P, 2, BLOCK], F32, name="pos_pair")
-                cap_pair = dpool.tile([P, 2, BLOCK], F32, name="cap_pair")
-                pairs[(blk, j // 2)] = (pos_pair, cap_pair, exp_pair)
-            pos_pair, cap_pair, exp_pair = pairs[(blk, j // 2)]
-            nc.scalar.activation(
-                out=exp_pair[:, j % 2, :], in_=pm[:], func=ACT.Exp, bias=exp2_bias[:, j : j + 1], scale=1.0,
-            )
-            nc.scalar.activation(
-                out=pos_pair[:, j % 2, :], in_=pm[:], func=ACT.Relu, bias=relu2_bias[:, j : j + 1], scale=1.0,
+                d_pair = dpool.tile([P, 2, BLOCK], F32, name="d_pair")
+                w_pair = wpool.tile([P, 2, BLOCK], F32, name="w_pair")
+                pairs[(blk, j // 2)] = (d_pair, w_pair)
+            d_pair, w_pair = pairs[(blk, j // 2)]
+            exp2 = act2.tile([P, BLOCK], F32, name="exp2")
+            pos = act2.tile([P, BLOCK], F32, name="pos")
+            nc.scalar.activation(out=exp2[:], in_=pm[:], func=ACT.Exp, bias=exp2_bias[:, j : j + 1], scale=1.0)
+            if j in VECTOR_RELU_TILES:
+                nc.vector.tensor_scalar(
+                    out=pos[:], in0=pm[:], scalar1=relu2_bias[:, j : j + 1], scalar2=0.0, op0=ALU.add, op1=ALU.max,
+                )
+            else:
+                nc.scalar.activation(out=pos[:], in_=pm[:], func=ACT.Relu, bias=relu2_bias[:, j : j + 1], scale=1.0)
+            nc.vector.scalar_tensor_tensor(
+                out=d_pair[:, j % 2, :], in0=exp2[:], scalar=-SELU_ALPHA, in1=pos[:], op0=ALU.add, op1=ALU.min,
             )
             if j % 2 == 1:
-                nc.vector.tensor_scalar(
-                    out=cap_pair[:], in0=exp_pair[:], scalar1=SELU_ALPHA, scalar2=-SELU_ALPHA, op0=ALU.min, op1=ALU.add,
-                )
+                nc.scalar.activation(out=w_pair[:], in_=d_pair[:], func=ACT.Abs)
 
         def turned(dest, blk, j, which, s, start, stop):
             nc.tensor.matmul(
@@ -303,27 +307,17 @@ def tile_basicemotionpredictions_pa_t_e_kernel(tc, h2, gamma, beta, Wh_words, Wh
 
         def norm_sums(blk, s):
             if s == 0:
-                sum_pos = sum_psum.tile([P, SUBS, P], F32, name="sum_pos")
-                sum_cap = sum_psum.tile([P, SUBS, P], F32, name="sum_cap")
-                sums2[blk] = (sum_pos, sum_cap)
-            for which in range(2):
-                for j in range(OUT_TILES):
-                    turned(sums2[blk][which][:, s, :], blk, j, which, s, j == 0, j == OUT_TILES - 1)
+                sums2[blk] = tv_psum.tile([P, SUBS, P], F32, name="sum_w", tag="values")
+            for j in range(OUT_TILES):
+                turned(sums2[blk][:, s, :], blk, j, 1, s, j == 0, j == OUT_TILES - 1)
 
         def norm_finish(blk):
-            sum_pos, sum_cap = sums2[blk]
-            l1_pos = small.tile([P, SUBS * HEADS], F32, name="l1_pos")
-            l1_cap = small.tile([P, SUBS * HEADS], F32, name="l1_cap")
             l1 = small.tile([P, SUBS * HEADS], F32, name="l1")
             l1_floor = small.tile([P, SUBS * HEADS], F32, name="l1_floor")
             inv = small.tile([P, SUBS, HEADS], F32, name="inv")
             nc.vector.tensor_reduce(
-                out=l1_pos[:], in_=sum_pos[:].rearrange("p s (m e) -> p (s m) e", e=E_LOW), axis=AXIS.X, op=ALU.add,
+                out=l1[:], in_=sums2[blk][:].rearrange("p s (m e) -> p (s m) e", e=E_LOW), axis=AXIS.X, op=ALU.add,
             )
-            nc.vector.tensor_reduce(
-                out=l1_cap[:], in_=sum_cap[:].rearrange("p s (m e) -> p (s m) e", e=E_LOW), axis=AXIS.X, op=ALU.add,
-            )
-            nc.vector.tensor_sub(out=l1[:], in0=l1_pos[:], in1=l1_cap[:])
             nc.vector.tensor_scalar_max(out=l1_floor[:], in0=l1[:], scalar1=L1_EPS / SELU_SCALE)
             nc.vector.reciprocal(out=inv[:].rearrange("p s m -> p (s m)"), in_=l1_floor[:])
             invs[blk] = inv
@@ -332,10 +326,7 @@ def tile_basicemotionpredictions_pa_t_e_kernel(tc, h2, gamma, beta, Wh_words, Wh
             rows = out_rows[blk * BLOCK : (blk + 1) * BLOCK, :].rearrange("(p s) n -> p s n", s=SUBS)
             values = tv_psum.tile([P, HALF_TILES, HEADS, E_LOW], F32, name="values")
             for jj in range(HALF_TILES):
-                for which in range(2):
-                    turned(
-                        values[:, jj].rearrange("p m e -> p (m e)"), blk, half * HALF_TILES + jj, which, s, which == 0, which == 1,
-                    )
+                turned(values[:, jj].rearrange("p m e -> p (m e)"), blk, half * HALF_TILES + jj, 0, s, True, True)
             if half == 0:
                 o = opool.tile([P, HEADS, HEAD], F32, name="o")
                 outs[(blk, s)] = o

@@ -70,7 +70,7 @@ def tile_basicemotionpredictions_pa_t_e_kernel(tc, h2, gamma, beta, Wh_words, Wh
             )
             x_blocks.append(x_blk)
 
-        for blk in range(4):
+        for blk in range(N_BLOCKS):
             load_x(blk)
 
         gamma_bf = const.tile([P, PASSES, PACK], BF16)
@@ -101,8 +101,6 @@ def tile_basicemotionpredictions_pa_t_e_kernel(tc, h2, gamma, beta, Wh_words, Wh
                     out=planes_raw[32 * quad : 32 * quad + 4, c, :].rearrange("r (m w) -> r m w", w=HEAD // 4),
                     in_=scales_dram[c, 4 * quad : 4 * quad + 4],
                 )
-        for blk in range(4, N_BLOCKS):
-            load_x(blk)
         for c in range(PASSES):
             nc.gpsimd.tensor_copy(
                 out=w_words[:, c, :].bitcast(I32).rearrange("p (j m e) -> p j m e", j=OUT_TILES, e=E_LOW),

@@ -322,18 +322,18 @@ def tile_basicemotionpredictions_pa_t_e_kernel(tc, h2, gamma, beta, Wh_words, Wh
 
         def normalise_and_store(blk, s, half):
             rows = out_rows[blk * BLOCK : (blk + 1) * BLOCK, :].rearrange("(p s) n -> p s n", s=SUBS)
-            values = tv_psum.tile([P, HALF_TILES, HEADS, E_LOW], F32, name="values")
+            values = tv_psum.tile([P, HEADS, HALF_TILES * E_LOW], F32, name="values")
             for jj in range(HALF_TILES):
-                turned(values[:, jj].rearrange("p m e -> p (m e)"), blk, half * HALF_TILES + jj, 0, s, True, True)
+                turned(values[:, :, jj * E_LOW : (jj + 1) * E_LOW], blk, half * HALF_TILES + jj, 0, s, True, True)
             if half == 0:
                 o = opool.tile([P, HEADS, HEAD], F32, name="o")
                 outs[(blk, s)] = o
             o = outs[(blk, s)]
             span = HALF_TILES * E_LOW
             nc.vector.tensor_tensor(
-                out=o[:, :, half * span : (half + 1) * span].rearrange("p m (j e) -> p m j e", e=E_LOW),
-                in0=values[:].rearrange("p j m e -> p m j e"),
-                in1=invs[blk][:, s, :].unsqueeze(2).unsqueeze(3).to_broadcast([P, HEADS, HALF_TILES, E_LOW]),
+                out=o[:, :, half * span : (half + 1) * span],
+                in0=values[:],
+                in1=invs[blk][:, s, :].unsqueeze(2).to_broadcast([P, HEADS, span]),
                 op=ALU.mult,
             )
             if half == 1:

@@ -29,6 +29,7 @@ OUT_TILES = OUTPUTS // P
 HALF_TILES = OUT_TILES // 2
 HEADS = OUTPUTS // HEAD
 E_LOW = HEAD // OUT_TILES
+AHEAD = 2
 VECTOR_RELU_TILES = (0, 1, 2)
 STAT_CHUNK = 512
 
@@ -57,8 +58,8 @@ def tile_basicemotionpredictions_pa_t_e_kernel(tc, h2, gamma, beta, Wh_words, Wh
         small = ctx.enter_context(tc.tile_pool(name="small", bufs=2))
         scrap = ctx.enter_context(tc.tile_pool(name="scrap", bufs=4))
         xt_psum = ctx.enter_context(tc.psum_pool(name="xt_psum", bufs=2))
-        pm_psum = ctx.enter_context(tc.psum_pool(name="pm_psum", bufs=2))
-        tv_psum = ctx.enter_context(tc.psum_pool(name="tv_psum", bufs=4))
+        pm_psum = ctx.enter_context(tc.psum_pool(name="pm_psum", bufs=3))
+        tv_psum = ctx.enter_context(tc.psum_pool(name="tv_psum", bufs=3))
 
         x_blocks = []
 
@@ -207,6 +208,7 @@ def tile_basicemotionpredictions_pa_t_e_kernel(tc, h2, gamma, beta, Wh_words, Wh
         branches = {}
         clamped = {}
         exps = {}
+        joined = {}
         e_mx = {}
         pairs = {}
         sums2 = {}
@@ -240,8 +242,9 @@ def tile_basicemotionpredictions_pa_t_e_kernel(tc, h2, gamma, beta, Wh_words, Wh
             )
             exps[(blk, c)] = expo
 
-        def quantise_e(blk, c):
+        def join_e(blk, c):
             grouped = act1.tile([P, BLOCK, PACK], BF16, name="grouped", align_bytes=64)
+            joined[(blk, c)] = grouped
             nc.vector.scalar_tensor_tensor(
                 out=grouped[:],
                 in0=branches[(blk, c)][:].rearrange("p t b -> p b t"),
@@ -250,6 +253,9 @@ def tile_basicemotionpredictions_pa_t_e_kernel(tc, h2, gamma, beta, Wh_words, Wh
                 op0=ALU.max,
                 op1=ALU.add,
             )
+
+        def quantise_e(blk, c):
+            grouped = joined[(blk, c)]
             e_words = quant.tile([P, BLOCK], U32, name="e_words", align_bytes=64)
             e_plane = quant.tile([P, BLOCK], U8, name="e_plane", align_bytes=64)
             nc.vector.quantize_mx(
@@ -339,24 +345,27 @@ def tile_basicemotionpredictions_pa_t_e_kernel(tc, h2, gamma, beta, Wh_words, Wh
             if half == 1:
                 nc.sync.dma_start(out=rows[:, s, :], in_=o[:].rearrange("p m e -> p (m e)"))
 
-        for blk in range(-1, N_BLOCKS + 1):
-            nxt = blk + 1
+        for step in range(-OUT_TILES - AHEAD, OUT_TILES * (N_BLOCKS + 1)):
+            blk, j = divmod(step, OUT_TILES)
+            nxt, je = divmod(step + OUT_TILES + AHEAD, OUT_TILES)
             prev = blk - 1
-            for j in range(OUT_TILES):
-                if j % 4 < 2 and nxt < N_BLOCKS:
-                    linear_branch(nxt, j // 4, j % 4)
-                if j % 4 == 1 and nxt < N_BLOCKS:
-                    clamp(nxt, j // 4)
-                if j % 4 == 2 and nxt < N_BLOCKS:
-                    exp_branch(nxt, j // 4)
-                if 0 <= blk < N_BLOCKS:
-                    heads(blk, j)
-                if j % 4 == 3 and nxt < N_BLOCKS:
-                    quantise_e(nxt, j // 4)
-                if prev >= 0 and j < SUBS:
-                    norm_sums(prev, j)
-                if prev >= 0 and j == SUBS - 1:
-                    norm_finish(prev)
-                if prev >= 0 and j >= SUBS:
-                    normalise_and_store(prev, j - SUBS, 0)
-                    normalise_and_store(prev, j - SUBS, 1)
+            qb, qe = divmod(step - 1 + OUT_TILES + AHEAD, OUT_TILES)
+            if je % 4 < 2 and nxt < N_BLOCKS:
+                linear_branch(nxt, je // 4, je % 4)
+            if je % 4 == 1 and nxt < N_BLOCKS:
+                clamp(nxt, je // 4)
+            if je % 4 == 2 and nxt < N_BLOCKS:
+                exp_branch(nxt, je // 4)
+            if 0 <= blk < N_BLOCKS:
+                heads(blk, j)
+            if qe % 4 == 3 and 0 <= qb < N_BLOCKS:
+                quantise_e(qb, qe // 4)
+            if je % 4 == 3 and nxt < N_BLOCKS:
+                join_e(nxt, je // 4)
+            if prev >= 0 and j < SUBS:
+                norm_sums(prev, j)
+            if prev >= 0 and j == SUBS - 1:
+                norm_finish(prev)
+            if prev >= 0 and j >= SUBS:
+                normalise_and_store(prev, j - SUBS, 0)
+                normalise_and_store(prev, j - SUBS, 1)

import math
from contextlib import ExitStack

import concourse.mybir as mybir
from concourse.masks import make_identity

F32 = mybir.dt.float32
BF16 = mybir.dt.bfloat16
I32 = mybir.dt.int32
U32 = mybir.dt.uint32
U8 = mybir.dt.uint8
FP8X4 = mybir.dt.float8_e4m3fn_x4
ACT = mybir.ActivationFunctionType
ALU = mybir.AluOpType
AXIS = mybir.AxisListType

P = 128
ROWS = 4096
FEATURES = 1024
OUTPUTS = 1024
HEAD = 32
PACK = 4
K_PASS = P * PACK
PASSES = FEATURES // K_PASS
BLOCK = 512
SUBS = BLOCK // P
N_BLOCKS = ROWS // BLOCK
OUT_TILES = OUTPUTS // P
HALF_TILES = OUT_TILES // 2
HEADS = OUTPUTS // HEAD
E_LOW = HEAD // OUT_TILES
AHEAD = 2
VECTOR_RELU_TILES = (0, 1, 2)
STAT_CHUNK = 512

BN_EPS = 1e-5
L1_EPS = 1e-12
SELU_ALPHA = 1.6732632423543772
SELU_SCALE = 1.0507009873554805
SCALE_ALPHA = SELU_SCALE * SELU_ALPHA

FLOPS = 2 * ROWS * FEATURES * OUTPUTS


def tile_basicemotionpredictions_pa_t_e_kernel(tc, h2, gamma, beta, Wh_words, Wh_scales, bh, out):
    nc = tc.nc
    out_rows = out.rearrange("b h g e -> b (h g e)")

    with ExitStack() as ctx:
        const = ctx.enter_context(tc.tile_pool(name="const", bufs=1))
        xpool = ctx.enter_context(tc.tile_pool(name="x", bufs=1))
        act1 = ctx.enter_context(tc.tile_pool(name="act1", bufs=2))
        quant = ctx.enter_context(tc.tile_pool(name="quant", bufs=4))
        act2 = ctx.enter_context(tc.tile_pool(name="act2", bufs=3))
        dpool = ctx.enter_context(tc.tile_pool(name="d", bufs=OUT_TILES))
        wpool = ctx.enter_context(tc.tile_pool(name="w", bufs=6))
        opool = ctx.enter_context(tc.tile_pool(name="o", bufs=3))
        small = ctx.enter_context(tc.tile_pool(name="small", bufs=2))
        scrap = ctx.enter_context(tc.tile_pool(name="scrap", bufs=4))
        xt_psum = ctx.enter_context(tc.psum_pool(name="xt_psum", bufs=2))
        pm_psum = ctx.enter_context(tc.psum_pool(name="pm_psum", bufs=3))
        tv_psum = ctx.enter_context(tc.psum_pool(name="tv_psum", bufs=3))

        x_blocks = []

        def load_x(blk):
            x_blk = xpool.tile([P, SUBS, FEATURES], BF16, name="x%d" % blk)
            nc.sync.dma_start(
                out=x_blk[:],
                in_=h2[blk * BLOCK : (blk + 1) * BLOCK, :].rearrange("(p s) k -> p s k", s=SUBS),
            )
            x_blocks.append(x_blk)

        for blk in range(N_BLOCKS):
            load_x(blk)

        gamma_bf = const.tile([P, PASSES, PACK], BF16)
        beta_bf = const.tile([P, PASSES, PACK], BF16)
        nc.scalar.dma_start(out=gamma_bf[:], in_=gamma.rearrange("(c p t) -> p c t", c=PASSES, t=PACK))
        nc.scalar.dma_start(out=beta_bf[:], in_=beta.rearrange("(c p t) -> p c t", c=PASSES, t=PACK))
        bh_bf = const.tile([P, OUT_TILES], BF16)
        bh_heads = bh.rearrange("h g e -> (h g) e")
        with nc.allow_non_contiguous_dma(reason="1,024 bias values, one to a partition and column"):
            for e in range(E_LOW):
                nc.scalar.dma_start(out=bh_bf[e:P:E_LOW, :], in_=bh_heads[:, e:HEAD:E_LOW])

        ident = const.tile([P, P], F32)
        make_identity(nc, ident[:])

        w_raw = act1.tile([P, PASSES, OUTPUTS], I32, name="w_raw", tag="lin")
        planes_raw = act1.tile([P, PASSES, OUTPUTS // 4], I32, name="planes_raw", tag="neg")
        w_words = const.tile([P, PASSES, OUTPUTS], U32, align_bytes=64)
        w_planes = const.tile([P, PASSES, OUTPUTS], U8, align_bytes=64)
        nc.vector.memset(planes_raw[:].rearrange("p c n -> p (c n)"), 0)
        words_dram = Wh_words.rearrange("g p n t -> g p (n t)").bitcast(I32).rearrange("(m c) p n -> c p m n", c=PASSES)
        scales_dram = Wh_scales.bitcast(I32).rearrange("(m c) q w -> c q m w", c=PASSES)
        for c in range(PASSES):
            nc.sync.dma_start(out=w_raw[:, c, :].rearrange("p (m n) -> p m n", n=HEAD), in_=words_dram[c])
        for c in range(PASSES):
            for quad in range(4):
                nc.sync.dma_start(
                    out=planes_raw[32 * quad : 32 * quad + 4, c, :].rearrange("r (m w) -> r m w", w=HEAD // 4),
                    in_=scales_dram[c, 4 * quad : 4 * quad + 4],
                )
        for c in range(PASSES):
            nc.gpsimd.tensor_copy(
                out=w_words[:, c, :].bitcast(I32).rearrange("p (j m e) -> p j m e", j=OUT_TILES, e=E_LOW),
                in_=w_raw[:, c, :].rearrange("p (m j e) -> p j m e", j=OUT_TILES, e=E_LOW),
            )
            nc.gpsimd.tensor_copy(
                out=w_planes[:, c, :].bitcast(I32).rearrange("p (j m) -> p j m", j=OUT_TILES),
                in_=planes_raw[:, c, :].rearrange("p (m j) -> p j m", j=OUT_TILES),
            )

        warm_in = const.tile([P, 1], F32)
        warm_sqrt = const.tile([P, 1], F32)
        warm_exp = const.tile([P, 1], F32)
        nc.vector.memset(warm_in[:], 1.0)
        nc.scalar.activation(out=warm_sqrt[:], in_=warm_in[:], func=ACT.Sqrt)

        def transpose_features(blk, c, u, pool, tag):
            x_words = x_blocks[blk][:].bitcast(F32)
            xt = pool.tile([P, BLOCK], F32, name="xt", tag=tag)
            for s in range(SUBS):
                nc.tensor.transpose(
                    out=xt[:, s * P : (s + 1) * P],
                    in_=x_words[:, s, 256 * c + u : 256 * (c + 1) : 2],
                    identity=ident[:],
                )
            return xt

        chunks = N_BLOCKS * 2 * BLOCK // STAT_CHUNK
        vector_banks = 2 * PASSES - 1
        n_feat = PASSES * PACK
        stats = const.tile([P, vector_banks, chunks, 6], F32)
        neg_pivot = const.tile([P, 2], F32)
        sums = const.tile([P, 2, 2, N_BLOCKS], F32)
        for blk in range(N_BLOCKS):
            for c in range(PASSES):
                for u in range(2):
                    if 2 * c + u < vector_banks:
                        xt = transpose_features(blk, c, u, xt_psum, "xt")
                    else:
                        xt = transpose_features(blk, c, u, tv_psum, "values")
                    pairs = xt[:].bitcast(BF16)
                    if 2 * c + u < vector_banks:
                        for h in range(2):
                            nc.vector.bn_stats(
                                out=stats[:, 2 * c + u, 2 * blk + h, :],
                                in_=pairs[:, h * STAT_CHUNK : (h + 1) * STAT_CHUNK],
                            )
                    else:
                        if blk == 0:
                            nc.vector.tensor_scalar_mul(out=neg_pivot[:], in0=pairs[:, 0:2], scalar1=-1.0)
                        by_feature = pairs.rearrange("p (b e) -> p b e", e=2)
                        for e in range(2):
                            centred = scrap.tile([P, BLOCK], BF16, name="centred")
                            squared = scrap.tile([P, BLOCK], BF16, name="squared")
                            nc.scalar.activation(
                                out=centred[:], in_=by_feature[:, :, e], func=ACT.Identity,
                                bias=neg_pivot[:, e : e + 1], scale=1.0, accum_out=sums[:, e, 0, blk : blk + 1],
                            )
                            nc.scalar.activation(
                                out=squared[:], in_=by_feature[:, :, e], func=ACT.Square,
                                bias=neg_pivot[:, e : e + 1], scale=1.0, accum_out=sums[:, e, 1, blk : blk + 1],
                            )
        mean_var = const.tile([P, n_feat, 2], F32)
        for cu in range(vector_banks):
            for e in range(2):
                nc.vector.bn_aggr(out=mean_var[:, 2 * cu + e, :], in_=stats[:, cu, :, 3 * e : 3 * e + 3])
        moments = const.tile([P, 2, 2], F32)
        m1_squared = const.tile([P, 2], F32)
        nc.vector.tensor_reduce(out=moments[:], in_=sums[:], axis=AXIS.X, op=ALU.add)
        nc.vector.tensor_scalar_mul(out=moments[:], in0=moments[:], scalar1=1.0 / ROWS)
        nc.vector.tensor_sub(out=mean_var[:, 2 * vector_banks :, 0], in0=moments[:, :, 0], in1=neg_pivot[:])
        nc.vector.tensor_mul(out=m1_squared[:], in0=moments[:, :, 0], in1=moments[:, :, 0])
        nc.vector.tensor_sub(out=mean_var[:, 2 * vector_banks :, 1], in0=moments[:, :, 1], in1=m1_squared[:])

        var_eps = const.tile([P, n_feat], F32)
        std = const.tile([P, n_feat], F32)
        rstd = const.tile([P, n_feat], F32)
        gain = const.tile([P, n_feat], F32)
        mean_gain = const.tile([P, n_feat], F32)
        shift = const.tile([P, n_feat], F32)
        lin_scale = const.tile([P, n_feat], F32)
        lin_bias = const.tile([P, n_feat], F32)
        zero = const.tile([P, 1], F32)
        exp1_bias = const.tile([P, 1], F32)
        nc.vector.tensor_scalar_add(out=var_eps[:], in0=mean_var[:, :, 1], scalar1=BN_EPS)
        nc.scalar.activation(out=std[:], in_=var_eps[:], func=ACT.Sqrt)
        nc.scalar.activation(out=warm_exp[:], in_=std[:, 0:1], func=ACT.Exp)
        nc.vector.reciprocal(out=rstd[:], in_=std[:])
        nc.vector.tensor_mul(out=gain[:], in0=rstd[:], in1=gamma_bf[:].rearrange("p c t -> p (c t)"))
        nc.vector.tensor_mul(out=mean_gain[:], in0=mean_var[:, :, 0], in1=gain[:])
        nc.vector.tensor_sub(out=shift[:], in0=beta_bf[:].rearrange("p c t -> p (c t)"), in1=mean_gain[:])
        nc.vector.tensor_scalar_mul(out=lin_scale[:], in0=gain[:], scalar1=SELU_SCALE)
        nc.vector.tensor_scalar(
            out=lin_bias[:], in0=shift[:], scalar1=SELU_SCALE, scalar2=-SCALE_ALPHA, op0=ALU.mult, op1=ALU.add,
        )
        nc.vector.memset(zero[:], 0.0)
        nc.vector.tensor_scalar_add(out=exp1_bias[:], in0=zero[:], scalar1=SELU_ALPHA + math.log(SCALE_ALPHA))

        relu2_bias = const.tile([P, OUT_TILES], F32)
        exp2_bias = const.tile([P, OUT_TILES], F32)
        nc.vector.tensor_copy(out=relu2_bias[:], in_=bh_bf[:])
        nc.vector.tensor_scalar_add(out=exp2_bias[:], in0=bh_bf[:], scalar1=math.log(SELU_ALPHA))

        branches = {}
        clamped = {}
        exps = {}
        joined = {}
        e_mx = {}
        pairs = {}
        sums2 = {}
        invs = {}
        outs = {}

        def linear_branch(blk, c, u):
            if u == 0:
                lin = act1.tile([P, PACK, BLOCK], F32, name="lin")
                branches[(blk, c)] = lin
            lin = branches[(blk, c)]
            xt = transpose_features(blk, c, u, xt_psum, "xt")
            pairs = xt[:].bitcast(BF16).rearrange("p (b e) -> p b e", e=2)
            for e in range(2):
                t = 2 * u + e
                f = PACK * c + t
                nc.scalar.activation(
                    out=lin[:, t, :], in_=pairs[:, :, e], func=ACT.Identity,
                    bias=lin_bias[:, f : f + 1], scale=lin_scale[:, f : f + 1],
                )

        def clamp(blk, c):
            neg = act1.tile([P, PACK, BLOCK], F32, name="neg")
            nc.vector.tensor_scalar_min(out=neg[:], in0=branches[(blk, c)][:], scalar1=-SCALE_ALPHA)
            clamped[(blk, c)] = neg

        def exp_branch(blk, c):
            expo = clamped[(blk, c)]
            nc.scalar.activation(
                out=expo[:], in_=expo[:], func=ACT.Exp, bias=exp1_bias[:, 0:1], scale=1.0 / SELU_SCALE,
            )
            exps[(blk, c)] = expo

        def join_e(blk, c):
            grouped = act1.tile([P, BLOCK, PACK], BF16, name="grouped", align_bytes=64)
            joined[(blk, c)] = grouped
            nc.vector.scalar_tensor_tensor(
                out=grouped[:],
                in0=branches[(blk, c)][:].rearrange("p t b -> p b t"),
                scalar=-SCALE_ALPHA,
                in1=exps[(blk, c)][:].rearrange("p t b -> p b t"),
                op0=ALU.max,
                op1=ALU.add,
            )

        def quantise_e(blk, c):
            grouped = joined[(blk, c)]
            e_words = quant.tile([P, BLOCK], U32, name="e_words", align_bytes=64)
            e_plane = quant.tile([P, BLOCK], U8, name="e_plane", align_bytes=64)
            nc.vector.quantize_mx(
                out=e_words[:].bitcast(FP8X4),
                scales=e_plane[:],
                in_=grouped[:].rearrange("p b t -> p (b t)"),
            )
            e_mx[(blk, c)] = (e_words, e_plane)

        def heads(blk, j):
            cols = slice(j * P, (j + 1) * P)
            pm = pm_psum.tile([P, BLOCK], F32, name="pm")
            for c in range(PASSES):
                e_words, e_plane = e_mx[(blk, c)]
                nc.tensor.matmul_mx(
                    out=pm[:],
                    lhsT=w_words[:, c, cols].bitcast(FP8X4),
                    lhsT_scale=w_planes[:, c, cols],
                    rhs=e_words[:].bitcast(FP8X4),
                    rhs_scale=e_plane[:],
                    start=(c == 0),
                    stop=(c == PASSES - 1),
                )
            if j % 2 == 0:
                d_pair = dpool.tile([P, 2, BLOCK], F32, name="d_pair")
                w_pair = wpool.tile([P, 2, BLOCK], F32, name="w_pair")
                pairs[(blk, j // 2)] = (d_pair, w_pair)
            d_pair, w_pair = pairs[(blk, j // 2)]
            exp2 = act2.tile([P, BLOCK], F32, name="exp2")
            pos = act2.tile([P, BLOCK], F32, name="pos")
            nc.scalar.activation(out=exp2[:], in_=pm[:], func=ACT.Exp, bias=exp2_bias[:, j : j + 1], scale=1.0)
            if j in VECTOR_RELU_TILES:
                nc.vector.tensor_scalar(
                    out=pos[:], in0=pm[:], scalar1=relu2_bias[:, j : j + 1], scalar2=0.0, op0=ALU.add, op1=ALU.max,
                )
            else:
                nc.scalar.activation(out=pos[:], in_=pm[:], func=ACT.Relu, bias=relu2_bias[:, j : j + 1], scale=1.0)
            nc.vector.scalar_tensor_tensor(
                out=d_pair[:, j % 2, :], in0=exp2[:], scalar=-SELU_ALPHA, in1=pos[:], op0=ALU.add, op1=ALU.min,
            )
            if j % 2 == 1:
                nc.scalar.activation(out=w_pair[:], in_=d_pair[:], func=ACT.Abs)

        def turned(dest, blk, j, which, s, start, stop):
            nc.tensor.matmul(
                out=dest,
                lhsT=pairs[(blk, j // 2)][which][:, j % 2, s * P : (s + 1) * P],
                rhs=ident[:],
                is_transpose=True,
                start=start,
                stop=stop,
            )

        def norm_sums(blk, s):
            if s == 0:
                sums2[blk] = tv_psum.tile([P, SUBS, P], F32, name="sum_w", tag="values")
            for j in range(OUT_TILES):
                turned(sums2[blk][:, s, :], blk, j, 1, s, j == 0, j == OUT_TILES - 1)

        def norm_finish(blk):
            l1 = small.tile([P, SUBS * HEADS], F32, name="l1")
            l1_floor = small.tile([P, SUBS * HEADS], F32, name="l1_floor")
            inv = small.tile([P, SUBS, HEADS], F32, name="inv")
            nc.vector.tensor_reduce(
                out=l1[:], in_=sums2[blk][:].rearrange("p s (m e) -> p (s m) e", e=E_LOW), axis=AXIS.X, op=ALU.add,
            )
            nc.vector.tensor_scalar_max(out=l1_floor[:], in0=l1[:], scalar1=L1_EPS / SELU_SCALE)
            nc.vector.reciprocal(out=inv[:].rearrange("p s m -> p (s m)"), in_=l1_floor[:])
            invs[blk] = inv

        def normalise_and_store(blk, s, half):
            rows = out_rows[blk * BLOCK : (blk + 1) * BLOCK, :].rearrange("(p s) n -> p s n", s=SUBS)
            values = tv_psum.tile([P, HEADS, HALF_TILES * E_LOW], F32, name="values")
            for jj in range(HALF_TILES):
                turned(values[:, :, jj * E_LOW : (jj + 1) * E_LOW], blk, half * HALF_TILES + jj, 0, s, True, True)
            if half == 0:
                o = opool.tile([P, HEADS, HEAD], F32, name="o")
                outs[(blk, s)] = o
            o = outs[(blk, s)]
            span = HALF_TILES * E_LOW
            nc.vector.tensor_tensor(
                out=o[:, :, half * span : (half + 1) * span],
                in0=values[:],
                in1=invs[blk][:, s, :].unsqueeze(2).to_broadcast([P, HEADS, span]),
                op=ALU.mult,
            )
            if half == 1:
                nc.sync.dma_start(out=rows[:, s, :], in_=o[:].rearrange("p m e -> p (m e)"))

        for step in range(-OUT_TILES - AHEAD, OUT_TILES * (N_BLOCKS + 1)):
            blk, j = divmod(step, OUT_TILES)
            nxt, je = divmod(step + OUT_TILES + AHEAD, OUT_TILES)
            prev = blk - 1
            qb, qe = divmod(step - 1 + OUT_TILES + AHEAD, OUT_TILES)
            if je % 4 < 2 and nxt < N_BLOCKS:
                linear_branch(nxt, je // 4, je % 4)
            if je % 4 == 1 and nxt < N_BLOCKS:
                clamp(nxt, je // 4)
            if je % 4 == 2 and nxt < N_BLOCKS:
                exp_branch(nxt, je // 4)
            if 0 <= blk < N_BLOCKS:
                heads(blk, j)
            if qe % 4 == 3 and 0 <= qb < N_BLOCKS:
                quantise_e(qb, qe // 4)
            if je % 4 == 3 and nxt < N_BLOCKS:
                join_e(nxt, je // 4)
            if prev >= 0 and j < SUBS:
                norm_sums(prev, j)
            if prev >= 0 and j == SUBS - 1:
                norm_finish(prev)
            if prev >= 0 and j >= SUBS:
                normalise_and_store(prev, j - SUBS, 0)
                normalise_and_store(prev, j - SUBS, 1)
